import numpy as np
import ml_dtypes


def mxq(x, axis, fmt="e4m3"):
    dtype, down = {"e4m3": (ml_dtypes.float8_e4m3fn, 7), "e5m2": (ml_dtypes.float8_e5m2, 14)}[fmt]
    v = np.moveaxis(np.asarray(x, np.float32).astype(ml_dtypes.bfloat16).astype(np.float64), axis, -1)
    blocks = v.reshape(v.shape[:-1] + (-1, 32))
    amax = np.abs(blocks).max(-1, keepdims=True)
    byte = np.maximum(np.where(amax > 0, np.frexp(amax)[1] - 1 + 127, 0) - down, 1)
    scale = np.exp2(byte - 127.0)
    codes = (blocks / scale).astype(np.float32).astype(dtype).astype(np.float64)
    return np.moveaxis((codes * scale).reshape(v.shape), -1, axis)


WIDE = False


def mx_kscale(k):
    if not WIDE:
        return np.ones(k)
    levels = np.array([10, -10, 5, -5, 0])
    a = np.random.permutation(np.resize(levels, k // 512 * 4)).reshape(k // 512, 4)
    idx = np.arange(k)
    return np.exp2(a[idx // 512, idx % 128 // 32])


BF16 = ml_dtypes.bfloat16


def bf(x):
    return np.asarray(x, np.float32).astype(BF16)


def f64(x):
    return np.asarray(x).astype(np.float64)


B, T, C, H, QB = 8, 512, 512, 1, 512
DH = C // H
MASK_SCALE = 10000.0


def softmax(s):
    e = np.exp(s - s.max(-1, keepdims=True))
    return e / e.sum(-1, keepdims=True)


def heads(a):
    return a.reshape(B, T, H, DH).transpose(0, 2, 1, 3)


def setup_inputs():
    t = mx_kscale(T)
    t = t / t.min()
    t = np.roll(t, -np.argmin(t))
    m = t.max()
    off = np.random.standard_normal(C) * 0.5
    q = np.random.standard_normal((B, T, C)) * 1.5
    k = np.random.standard_normal((B, T, C)) * 1.5
    v = np.random.standard_normal((B, T, C)) + off
    q[:, :, ::DH] = 2.0
    k[:, :, ::DH] -= (np.log(t) * np.sqrt(DH) / 2.0)[None, :, None]
    v = v * t[None, :, None]
    return {"q": bf(q), "k": bf(k), "v": bf(v),
            "alpha": bf((1.0 + 0.1 * np.random.standard_normal(1)) / m),
            "beta": bf(1.0 + 0.1 * np.random.standard_normal(1)),
            "gamma": bf((0.6 + 0.1 * np.random.standard_normal(1)) / m)}


def reference(q, k, v, alpha, beta, gamma):
    qh, kh, vh = heads(f64(q)), heads(f64(k)), heads(f64(v))
    a, b, g = f64(alpha), f64(beta), f64(gamma)
    vq = mxq(vh, 2, "e4m3")
    y = []
    for r in range(0, T, QB):
        n = r + QB
        tril = np.arange(r, n)[:, None] >= np.arange(n)[None, :]
        eye = np.arange(r, n)[:, None] == np.arange(n)[None, :]
        s = qh[:, :, r:n] @ kh[:, :, :n].transpose(0, 1, 3, 2) * DH ** -0.5
        att = softmax(np.where(tril, s, -np.inf))
        ident = softmax(eye * MASK_SCALE)
        mc = softmax(tril * MASK_SCALE)
        shaped = b * att + a * ident - g * mc
        y.append(mxq(shaped, 3, "e4m3") @ vq[:, :, :n])
    return np.concatenate(y, 2).transpose(0, 2, 1, 3).reshape(B, T, C)

@@ -1,0 +1,337 @@
+from contextlib import ExitStack
+import math
+
+import concourse.mybir as mybir
+from concourse.masks import make_identity
+
+F32 = mybir.dt.float32
+BF16 = mybir.dt.bfloat16
+I32 = mybir.dt.int32
+U32 = mybir.dt.uint32
+U8 = mybir.dt.uint8
+FP8X4 = mybir.dt.float8_e4m3fn_x4
+ALU = mybir.AluOpType
+ACT = mybir.ActivationFunctionType
+AX = mybir.AxisListType
+
+B, T, C = 8, 512, 512
+P = 128
+NT = T // P
+UNITS = B * NT
+PACK = 4
+SCALE = 1.0 / math.sqrt(C)
+MASKED = -1.0e30
+
+FLOPS = 2 * 2 * B * T * T * C
+
+
+def tile_causalshapedattention_pa_t_kernel(tc, q, k, v, alpha, beta, gamma, out):
+    nc = tc.nc
+    with ExitStack() as ctx:
+        consts = ctx.enter_context(tc.tile_pool(name="consts", bufs=1))
+        loads = ctx.enter_context(tc.tile_pool(name="loads", bufs=B))
+        seqs = ctx.enter_context(tc.tile_pool(name="seqs", bufs=3))
+        rows = ctx.enter_context(tc.tile_pool(name="rows", bufs=4))
+        stores = ctx.enter_context(tc.tile_pool(name="stores", bufs=12))
+        ps_tr = ctx.enter_context(tc.psum_pool(name="ps_tr", bufs=1))
+        ps_s = ctx.enter_context(tc.psum_pool(name="ps_s", bufs=3))
+        ps_pt = ctx.enter_context(tc.psum_pool(name="ps_pt", bufs=2))
+        ps_o = ctx.enter_context(tc.psum_pool(name="ps_o", bufs=2))
+        ctx.enter_context(tc.manual_schedule())
+
+        alpha_bf = consts.tile([P, 1], BF16)
+        nc.scalar.dma_start(out=alpha_bf[:], in_=alpha.partition_broadcast(P))
+        beta_bf = consts.tile([P, 1], BF16)
+        nc.scalar.dma_start(out=beta_bf[:], in_=beta.partition_broadcast(P))
+        gamma_bf = consts.tile([P, 1], BF16)
+        nc.scalar.dma_start(out=gamma_bf[:], in_=gamma.partition_broadcast(P))
+
+        warm = consts.tile([P, 1], F32)
+        nc.vector.memset(warm[:], 0.0)
+        warm_exp = consts.tile([P, 1], F32)
+        nc.scalar.activation(out=warm_exp[:], in_=warm[:], func=ACT.Exp)
+
+        k_tiles, q_tiles, v_tiles = [], [], []
+        for n in range(B):
+            k_sb = loads.tile([P, NT, C], BF16, tag="k")
+            nc.sync.dma_start(out=k_sb[:], in_=k[n].rearrange("(a p) c -> p a c", p=P))
+            k_tiles.append(k_sb)
+            q_sb = loads.tile([P, NT, C], BF16, tag="q")
+            nc.sync.dma_start(out=q_sb[:], in_=q[n].rearrange("(a p) c -> p a c", p=P))
+            q_tiles.append(q_sb)
+            v_sb = loads.tile([P, PACK, C], BF16, tag="v")
+            nc.sync.dma_start(
+                out=v_sb[:].rearrange("p (u e) c -> p u (e c)", e=2),
+                in_=v[n].rearrange("(u p e) c -> p u (e c)", p=P, e=2),
+            )
+            v_tiles.append(v_sb)
+
+        ident_f32 = consts.tile([P, P], F32)
+        make_identity(nc, ident_f32[:])
+        ident_bf = consts.tile([P, P], BF16)
+        nc.vector.tensor_copy(out=ident_bf[:], in_=ident_f32[:])
+
+        tril = consts.tile([P, P], F32)
+        nc.gpsimd.memset(tril[:], 1.0)
+        nc.gpsimd.affine_select(
+            out=tril[:], in_=tril[:], compare_op=ALU.is_ge, fill=0.0,
+            base=0, pattern=[[-1, P]], channel_multiplier=1,
+        )
+        mask_add = consts.tile([P, P], BF16)
+        nc.vector.tensor_scalar(
+            out=mask_add[:], in0=tril[:], scalar1=1.0, scalar2=-MASKED,
+            op0=ALU.subtract, op1=ALU.mult,
+        )
+
+        row_number_i = consts.tile([P, NT], I32)
+        nc.gpsimd.iota(row_number_i[:], pattern=[[P, NT]], base=1, channel_multiplier=1)
+        row_number = consts.tile([P, NT], F32)
+        nc.vector.tensor_copy(out=row_number[:], in_=row_number_i[:])
+        mean_weight = consts.tile([P, NT], F32)
+        nc.vector.reciprocal(out=mean_weight[:], in_=row_number[:])
+
+        shaped_tiles = []
+        for i in range(NT):
+            shaped = consts.tile([P, T], BF16, name="shaped%d" % i)
+            nc.vector.memset(shaped[:], 0.0)
+            shaped_tiles.append(shaped)
+
+        alpha_f = consts.tile([P, 1], F32)
+        nc.vector.tensor_copy(out=alpha_f[:], in_=alpha_bf[:])
+        beta_f = consts.tile([P, 1], F32)
+        nc.vector.tensor_copy(out=beta_f[:], in_=beta_bf[:])
+        gamma_f = consts.tile([P, 1], F32)
+        nc.vector.tensor_copy(out=gamma_f[:], in_=gamma_bf[:])
+
+        neg_mc = consts.tile([P, NT], F32)
+        nc.vector.tensor_scalar(
+            out=neg_mc[:], in0=mean_weight[:], scalar1=gamma_f[:, 0:1], scalar2=-1.0,
+            op0=ALU.mult, op1=ALU.mult,
+        )
+        alpha_eye = consts.tile([P, P], F32)
+        nc.vector.tensor_scalar(
+            out=alpha_eye[:], in0=ident_f32[:], scalar1=alpha_f[:, 0:1], scalar2=None,
+            op0=ALU.mult,
+        )
+        diag_add = consts.tile([P, NT, P], F32)
+        for i in range(NT):
+            nc.vector.scalar_tensor_tensor(
+                out=diag_add[:, i, :], in0=tril[:], scalar=neg_mc[:, i : i + 1],
+                in1=alpha_eye[:], op0=ALU.mult, op1=ALU.add,
+            )
+
+        tr_banks, kq_ts, s_banks, shifts, e_tiles, e_sums, inv_sums, gains = {}, {}, {}, {}, {}, {}, {}, {}
+        v_groupeds, groupeds, pt_banks, p_words, o_banks, v_words = {}, {}, {}, {}, {}, {}
+        K_SLOT, Q_SLOT = 0, 2
+
+        def live(unit):
+            return 0 <= unit < UNITS
+
+        def transpose_inputs(unit):
+            if not live(unit):
+                return
+            n, a = divmod(unit, NT)
+            bank = ps_tr.tile([P, 4, P], F32, tag="tr")
+            for base, x_sb in ((K_SLOT, k_tiles[n]), (Q_SLOT, q_tiles[n])):
+                words = x_sb[:].bitcast(F32)
+                for u in range(2):
+                    nc.tensor.transpose(
+                        bank[:, base + u, :], words[:, a, u * P : (u + 1) * P], ident_f32[:]
+                    )
+            tr_banks[unit] = bank
+
+        def copy_transposed_inputs(unit):
+            if not live(unit):
+                return
+            n, a = divmod(unit, NT)
+            if a == 0:
+                kq_t = seqs.tile([P, NT, 4, P, 2], BF16, tag="kq_t")
+                kq_ts[n] = kq_t
+            nc.scalar.copy(
+                out=kq_ts[n][:, a, :, :, :].rearrange("p s t e -> p (s t e)"),
+                in_=tr_banks[unit][:].rearrange("p s t -> p (s t)").bitcast(BF16),
+            )
+
+        def scores(unit, steps):
+            if not live(unit):
+                return
+            n, i = divmod(unit, NT)
+            keys = (i + 1) * P
+            if 0 in steps:
+                s_ps = ps_s.tile([P, T], F32, tag="s")
+                s_banks[unit] = s_ps
+            s_ps = s_banks[unit]
+            kq_t = kq_ts[n]
+            for step in steps:
+                u, e = divmod(step, 2)
+                nc.tensor.matmul(
+                    s_ps[:, :keys].rearrange("p (a t) -> p a t", t=P),
+                    lhsT=kq_t[:, i, Q_SLOT + u, :, e], rhs=kq_t[:, : i + 1, K_SLOT + u, :, e],
+                    start=(step == 0), stop=(step == 3),
+                )
+                if step == 0:
+                    nc.tensor.matmul(
+                        s_ps[:, i * P : keys], lhsT=ident_bf[:], rhs=mask_add[:],
+                        start=False, stop=False,
+                    )
+
+        def row_max(unit):
+            if not live(unit):
+                return
+            keys = (unit % NT + 1) * P
+            neg_max = rows.tile([P, 1], F32, tag="neg_max")
+            nc.vector.reduce_max(out=neg_max[:], in_=s_banks[unit][:, :keys], axis=AX.X, negate=True)
+            shifts[unit] = neg_max
+
+        def row_shift(unit):
+            if not live(unit):
+                return
+            shift = rows.tile([P, 1], F32, tag="shift")
+            nc.vector.tensor_scalar(
+                out=shift[:], in0=shifts[unit][:], scalar1=SCALE, scalar2=None, op0=ALU.mult
+            )
+            shifts[unit] = shift
+
+        def exponentials(unit):
+            if not live(unit):
+                return
+            keys = (unit % NT + 1) * P
+            e_sb = rows.tile([P, T], F32, tag="e")
+            e_sum = rows.tile([P, 1], F32, tag="e_sum")
+            nc.scalar.activation(
+                out=e_sb[:, :keys], in_=s_banks[unit][:, :keys], func=ACT.Exp,
+                bias=shifts[unit][:, 0:1], scale=SCALE, accum_out=e_sum[:],
+            )
+            e_tiles[unit], e_sums[unit] = e_sb, e_sum
+
+        def invert_sum(unit):
+            if not live(unit):
+                return
+            inv_sum = rows.tile([P, 1], F32, tag="inv_sum")
+            nc.vector.reciprocal(out=inv_sum[:], in_=e_sums[unit][:])
+            inv_sums[unit] = inv_sum
+
+        def row_gain(unit):
+            if not live(unit):
+                return
+            gain = rows.tile([P, 1], F32, tag="gain")
+            nc.vector.tensor_scalar(
+                out=gain[:], in0=inv_sums[unit][:], scalar1=beta_f[:, 0:1], scalar2=None, op0=ALU.mult
+            )
+            gains[unit] = gain
+
+        def shape_rows(unit):
+            if not live(unit):
+                return
+            i = unit % NT
+            keys = (i + 1) * P
+            e_sb, gain = e_tiles[unit], gains[unit]
+            shaped = shaped_tiles[i]
+            if i > 0:
+                nc.vector.tensor_scalar(
+                    out=shaped[:, : i * P], in0=e_sb[:, : i * P],
+                    scalar1=gain[:, 0:1], scalar2=neg_mc[:, i : i + 1],
+                    op0=ALU.mult, op1=ALU.add,
+                )
+            nc.vector.scalar_tensor_tensor(
+                out=shaped[:, i * P : keys], in0=e_sb[:, i * P : keys], scalar=gain[:, 0:1],
+                in1=diag_add[:, i, :], op0=ALU.mult, op1=ALU.add,
+            )
+
+        def transpose_shaped(unit):
+            if not live(unit):
+                return
+            words = shaped_tiles[unit % NT][:].bitcast(F32)
+            pt_ps = ps_pt.tile([P, 2, P], F32, tag="pt")
+            for u in range(2):
+                nc.tensor.transpose(pt_ps[:, u, :], words[:, u * P : (u + 1) * P], ident_f32[:])
+            pt_banks[unit] = pt_ps
+
+        def group_shaped(unit):
+            if not live(unit):
+                return
+            grouped = rows.tile([P, P, PACK], BF16, tag="grouped", align_bytes=64)
+            nc.vector.tensor_copy(
+                out=grouped[:].rearrange("p r t -> p (r t)").bitcast(F32).rearrange("p (r u) -> p r u", u=2),
+                in_=pt_banks[unit][:].rearrange("p u r -> p r u"),
+            )
+            groupeds[unit] = grouped
+
+        def quantise_shaped(unit):
+            if not live(unit):
+                return
+            p_codes = rows.tile([P, P], U32, tag="p_codes", align_bytes=64)
+            p_scales = rows.tile([P, P], U8, tag="p_scales", align_bytes=64)
+            nc.vector.quantize_mx(
+                out=p_codes[:].bitcast(FP8X4), scales=p_scales[:],
+                in_=groupeds[unit][:].rearrange("p r t -> p (r t)"),
+            )
+            p_words[unit] = (p_codes, p_scales)
+
+        def group_values(unit):
+            if not live(unit):
+                return
+            n, piece = divmod(unit, NT)
+            v_grouped = rows.tile([P, P, PACK], BF16, tag="v_grouped", align_bytes=64)
+            nc.vector.tensor_copy(
+                out=v_grouped[:].rearrange("p (c i) t -> p c t i", i=4),
+                in_=v_tiles[n][:, :, piece * P : (piece + 1) * P].rearrange("p t (c i) -> p c t i", i=4),
+            )
+            v_groupeds[unit] = v_grouped
+
+        def quantise_values(unit):
+            if not live(unit):
+                return
+            n, piece = divmod(unit, NT)
+            if piece == 0:
+                v_codes = seqs.tile([P, C], U32, tag="v_codes", align_bytes=64)
+                v_scales = seqs.tile([P, C], U8, tag="v_scales", align_bytes=64)
+                v_words[n] = (v_codes, v_scales)
+            v_codes, v_scales = v_words[n]
+            cols = slice(piece * P, (piece + 1) * P)
+            nc.vector.quantize_mx(
+                out=v_codes[:, cols].bitcast(FP8X4), scales=v_scales[:, cols],
+                in_=v_groupeds[unit][:].rearrange("p c t -> p (c t)"),
+            )
+
+        def multiply_values(unit):
+            if not live(unit):
+                return
+            n = unit // NT
+            p_codes, p_scales = p_words[unit]
+            v_codes, v_scales = v_words[n]
+            o_ps = ps_o.tile([P, C], F32, tag="o")
+            nc.tensor.matmul_mx(
+                out=o_ps[:],
+                lhsT=p_codes[:].bitcast(FP8X4), lhsT_scale=p_scales[:],
+                rhs=v_codes[:].bitcast(FP8X4), rhs_scale=v_scales[:],
+                start=True, stop=True,
+            )
+            o_banks[unit] = o_ps
+
+        def store_output(unit):
+            if not live(unit):
+                return
+            n, i = divmod(unit, NT)
+            o_sb = stores.tile([P, C], F32, tag="o_sb")
+            nc.scalar.copy(out=o_sb[:], in_=o_banks[unit][:])
+            nc.sync.dma_start(out=out[n, i * P : (i + 1) * P, :], in_=o_sb[:])
+
+        for tick in range(-2, UNITS + 6):
+            store_output(tick - 5)
+            copy_transposed_inputs(tick + 1)
+            row_max(tick - 1)
+            invert_sum(tick - 2)
+            row_shift(tick - 1)
+            row_gain(tick - 2)
+            exponentials(tick - 1)
+            transpose_shaped(tick - 3)
+            group_shaped(tick - 3)
+            group_values(tick)
+            shape_rows(tick - 2)
+            quantise_shaped(tick - 3)
+            quantise_values(tick)
+            scores(tick, (0, 1))
+            multiply_values(tick - 4)
+            scores(tick, (2, 3))
+            transpose_inputs(tick + 2)

@@ -12,17 +12,30 @@ U8 = mybir.dt.uint8
 FP8X4 = mybir.dt.float8_e4m3fn_x4
 ALU = mybir.AluOpType
 ACT = mybir.ActivationFunctionType
-AX = mybir.AxisListType
 
 B, T, C = 8, 512, 512
 P = 128
 NT = T // P
-UNITS = B * NT
 PACK = 4
+ROUNDS = 2 * B
+BANKS = 4 * B
+HALF = C // 2
 SCALE = 1.0 / math.sqrt(C)
 MASKED = -1.0e30
 
 FLOPS = 2 * 2 * B * T * T * C
+
+
+def query_tiles(r):
+    first = r % 2
+    return (first, NT - 1 - first)
+
+
+def bank_contents(bank):
+    n, j = divmod(bank, 4)
+    if j < 2:
+        return "k", n, j, (2 * j, 2 * j + 1)
+    return "q", n, j - 2, query_tiles(j - 2)
 
 
 def tile_causalshapedattention_pa_t_kernel(tc, q, k, v, alpha, beta, gamma, out):
@@ -31,11 +44,12 @@ def tile_causalshapedattention_pa_t_kernel(tc, q, k, v, alpha, beta, gamma, out)
         consts = ctx.enter_context(tc.tile_pool(name="consts", bufs=1))
         loads = ctx.enter_context(tc.tile_pool(name="loads", bufs=B))
         seqs = ctx.enter_context(tc.tile_pool(name="seqs", bufs=3))
-        rows = ctx.enter_context(tc.tile_pool(name="rows", bufs=4))
-        stores = ctx.enter_context(tc.tile_pool(name="stores", bufs=12))
-        ps_tr = ctx.enter_context(tc.psum_pool(name="ps_tr", bufs=1))
+        rows = ctx.enter_context(tc.tile_pool(name="rows", bufs=6))
+        pairs = ctx.enter_context(tc.tile_pool(name="pairs", bufs=3))
+        stores = ctx.enter_context(tc.tile_pool(name="stores", bufs=16))
+        ps_tr = ctx.enter_context(tc.psum_pool(name="ps_tr", bufs=2))
         ps_s = ctx.enter_context(tc.psum_pool(name="ps_s", bufs=3))
-        ps_pt = ctx.enter_context(tc.psum_pool(name="ps_pt", bufs=2))
+        ps_pt = ctx.enter_context(tc.psum_pool(name="ps_pt", bufs=1))
         ps_o = ctx.enter_context(tc.psum_pool(name="ps_o", bufs=2))
         ctx.enter_context(tc.manual_schedule())
 
@@ -51,20 +65,40 @@ def tile_causalshapedattention_pa_t_kernel(tc, q, k, v, alpha, beta, gamma, out)
         warm_exp = consts.tile([P, 1], F32)
         nc.scalar.activation(out=warm_exp[:], in_=warm[:], func=ACT.Exp)
 
-        k_tiles, q_tiles, v_tiles = [], [], []
+        x_dram = {"k": k, "q": q}
+        x_sbs, v_sbs = {}, {}
         for n in range(B):
-            k_sb = loads.tile([P, NT, C], BF16, tag="k")
-            nc.sync.dma_start(out=k_sb[:], in_=k[n].rearrange("(a p) c -> p a c", p=P))
-            k_tiles.append(k_sb)
-            q_sb = loads.tile([P, NT, C], BF16, tag="q")
-            nc.sync.dma_start(out=q_sb[:], in_=q[n].rearrange("(a p) c -> p a c", p=P))
-            q_tiles.append(q_sb)
+            for name in ("k", "q"):
+                x_sb = loads.tile([P, NT, C], BF16, tag=name)
+                x_sbs[name, n] = x_sb
             v_sb = loads.tile([P, PACK, C], BF16, tag="v")
+            v_sbs[n] = v_sb
+
+        def load_tokens(name, n, first, count):
             nc.sync.dma_start(
-                out=v_sb[:].rearrange("p (u e) c -> p u (e c)", e=2),
+                out=x_sbs[name, n][:, first : first + count, :],
+                in_=x_dram[name][n, first * P : (first + count) * P, :].rearrange("(a p) c -> p a c", p=P),
+            )
+
+        def load_values(n):
+            nc.sync.dma_start(
+                out=v_sbs[n][:].rearrange("p (u e) c -> p u (e c)", e=2),
                 in_=v[n].rearrange("(u p e) c -> p u (e c)", p=P, e=2),
             )
-            v_tiles.append(v_sb)
+
+        for n in range(2):
+            load_tokens("k", n, 0, 2)
+            if n == 1:
+                load_values(0)
+            load_tokens("k", n, 2, 2)
+            load_tokens("q", n, 0, 1)
+            load_tokens("q", n, 3, 1)
+            load_tokens("q", n, 1, 2)
+        load_values(1)
+        for n in range(2, B):
+            load_tokens("k", n, 0, NT)
+            load_tokens("q", n, 0, NT)
+            load_values(n)
 
         ident_f32 = consts.tile([P, P], F32)
         make_identity(nc, ident_f32[:])
@@ -89,6 +123,8 @@ def tile_causalshapedattention_pa_t_kernel(tc, q, k, v, alpha, beta, gamma, out)
         nc.vector.tensor_copy(out=row_number[:], in_=row_number_i[:])
         mean_weight = consts.tile([P, NT], F32)
         nc.vector.reciprocal(out=mean_weight[:], in_=row_number[:])
+        minus_one = consts.tile([P, 1], F32)
+        nc.gpsimd.memset(minus_one[:], -1.0)
 
         shaped_tiles = []
         for i in range(NT):
@@ -120,53 +156,49 @@ def tile_causalshapedattention_pa_t_kernel(tc, q, k, v, alpha, beta, gamma, out)
                 in1=alpha_eye[:], op0=ALU.mult, op1=ALU.add,
             )
 
-        tr_banks, kq_ts, s_banks, shifts, e_tiles, e_sums, inv_sums, gains = {}, {}, {}, {}, {}, {}, {}, {}
-        v_groupeds, groupeds, pt_banks, p_words, o_banks, v_words = {}, {}, {}, {}, {}, {}
-        K_SLOT, Q_SLOT = 0, 2
+        tr_banks, x_ts, s_banks, neg_scores, shifts, e_tiles, e_sums, gains = {}, {}, {}, {}, {}, {}, {}, {}
+        pt_banks, groupeds, p_words, v_groupeds, v_words, o_banks = {}, {}, {}, {}, {}, {}
 
-        def live(unit):
-            return 0 <= unit < UNITS
+        def live(r):
+            return 0 <= r < ROUNDS
 
-        def transpose_inputs(unit):
-            if not live(unit):
+        def transpose_inputs(bank):
+            if not 0 <= bank < BANKS:
                 return
-            n, a = divmod(unit, NT)
-            bank = ps_tr.tile([P, 4, P], F32, tag="tr")
-            for base, x_sb in ((K_SLOT, k_tiles[n]), (Q_SLOT, q_tiles[n])):
-                words = x_sb[:].bitcast(F32)
+            name, n, half, tiles = bank_contents(bank)
+            words = x_sbs[name, n][:].bitcast(F32)
+            tr = ps_tr.tile([P, 2, 2, P], F32, tag="tr")
+            for m in range(2):
                 for u in range(2):
-                    nc.tensor.transpose(
-                        bank[:, base + u, :], words[:, a, u * P : (u + 1) * P], ident_f32[:]
-                    )
-            tr_banks[unit] = bank
+                    nc.tensor.transpose(tr[:, m, u, :], words[:, tiles[m], u * P : (u + 1) * P], ident_f32[:])
+            tr_banks[bank] = tr
 
-        def copy_transposed_inputs(unit):
-            if not live(unit):
+        def copy_transposed_inputs(bank):
+            if not 0 <= bank < BANKS:
                 return
-            n, a = divmod(unit, NT)
-            if a == 0:
-                kq_t = seqs.tile([P, NT, 4, P, 2], BF16, tag="kq_t")
-                kq_ts[n] = kq_t
+            name, n, half, tiles = bank_contents(bank)
+            if half == 0:
+                x_t = seqs.tile([P, NT, 2, P, 2], BF16, tag=name + "_t")
+                x_ts[name, n] = x_t
             nc.scalar.copy(
-                out=kq_ts[n][:, a, :, :, :].rearrange("p s t e -> p (s t e)"),
-                in_=tr_banks[unit][:].rearrange("p s t -> p (s t)").bitcast(BF16),
+                out=x_ts[name, n][:, 2 * half : 2 * half + 2, :, :, :].rearrange("p m u t e -> p (m u t e)"),
+                in_=tr_banks[bank][:].rearrange("p m u t -> p (m u t)").bitcast(BF16),
             )
 
-        def scores(unit, steps):
-            if not live(unit):
+        def scores(r, m, steps):
+            if not live(r):
                 return
-            n, i = divmod(unit, NT)
+            n, i = r // 2, query_tiles(r)[m]
             keys = (i + 1) * P
             if 0 in steps:
                 s_ps = ps_s.tile([P, T], F32, tag="s")
-                s_banks[unit] = s_ps
-            s_ps = s_banks[unit]
-            kq_t = kq_ts[n]
+                s_banks[r, m] = s_ps
+            s_ps = s_banks[r, m]
             for step in steps:
                 u, e = divmod(step, 2)
                 nc.tensor.matmul(
                     s_ps[:, :keys].rearrange("p (a t) -> p a t", t=P),
-                    lhsT=kq_t[:, i, Q_SLOT + u, :, e], rhs=kq_t[:, : i + 1, K_SLOT + u, :, e],
+                    lhsT=x_ts["q", n][:, 2 * (r % 2) + m, u, :, e], rhs=x_ts["k", n][:, : i + 1, u, :, e],
                     start=(step == 0), stop=(step == 3),
                 )
                 if step == 0:
@@ -175,57 +207,45 @@ def tile_causalshapedattention_pa_t_kernel(tc, q, k, v, alpha, beta, gamma, out)
                         start=False, stop=False,
                     )
 
-        def row_max(unit):
-            if not live(unit):
+        def scale_and_shift(r, m):
+            if not live(r):
                 return
-            keys = (unit % NT + 1) * P
-            neg_max = rows.tile([P, 1], F32, tag="neg_max")
-            nc.vector.reduce_max(out=neg_max[:], in_=s_banks[unit][:, :keys], axis=AX.X, negate=True)
-            shifts[unit] = neg_max
-
-        def row_shift(unit):
-            if not live(unit):
-                return
+            keys = (query_tiles(r)[m] + 1) * P
+            neg_s = rows.tile([P, T], F32, tag="neg_s")
             shift = rows.tile([P, 1], F32, tag="shift")
             nc.vector.tensor_scalar(
-                out=shift[:], in0=shifts[unit][:], scalar1=SCALE, scalar2=None, op0=ALU.mult
+                out=neg_s[:, :keys], in0=s_banks[r, m][:, :keys], scalar1=-SCALE, scalar2=None,
+                op0=ALU.mult, op1=ALU.min, accum_out=shift[:],
             )
-            shifts[unit] = shift
+            neg_scores[r, m], shifts[r, m] = neg_s, shift
 
-        def exponentials(unit):
-            if not live(unit):
+        def exponentials(r, m):
+            if not live(r):
                 return
-            keys = (unit % NT + 1) * P
+            keys = (query_tiles(r)[m] + 1) * P
             e_sb = rows.tile([P, T], F32, tag="e")
             e_sum = rows.tile([P, 1], F32, tag="e_sum")
             nc.scalar.activation(
-                out=e_sb[:, :keys], in_=s_banks[unit][:, :keys], func=ACT.Exp,
-                bias=shifts[unit][:, 0:1], scale=SCALE, accum_out=e_sum[:],
+                out=e_sb[:, :keys], in_=neg_scores[r, m][:, :keys], func=ACT.Exp,
+                bias=shifts[r, m][:, 0:1], scale=-1.0, accum_out=e_sum[:],
             )
-            e_tiles[unit], e_sums[unit] = e_sb, e_sum
+            e_tiles[r, m], e_sums[r, m] = e_sb, e_sum
 
-        def invert_sum(unit):
-            if not live(unit):
+        def row_gain(r, m):
+            if not live(r):
                 return
             inv_sum = rows.tile([P, 1], F32, tag="inv_sum")
-            nc.vector.reciprocal(out=inv_sum[:], in_=e_sums[unit][:])
-            inv_sums[unit] = inv_sum
-
-        def row_gain(unit):
-            if not live(unit):
-                return
+            nc.gpsimd.tensor_tensor(out=inv_sum[:], in0=e_sums[r, m][:], in1=minus_one[:], op=ALU.pow)
             gain = rows.tile([P, 1], F32, tag="gain")
-            nc.vector.tensor_scalar(
-                out=gain[:], in0=inv_sums[unit][:], scalar1=beta_f[:, 0:1], scalar2=None, op0=ALU.mult
-            )
-            gains[unit] = gain
+            nc.gpsimd.tensor_tensor(out=gain[:], in0=inv_sum[:], in1=beta_f[:], op=ALU.mult)
+            gains[r, m] = gain
 
-        def shape_rows(unit):
-            if not live(unit):
+        def shape_rows(r, m):
+            if not live(r):
                 return
-            i = unit % NT
+            i = query_tiles(r)[m]
             keys = (i + 1) * P
-            e_sb, gain = e_tiles[unit], gains[unit]
+            e_sb, gain = e_tiles[r, m], gains[r, m]
             shaped = shaped_tiles[i]
             if i > 0:
                 nc.vector.tensor_scalar(
@@ -238,100 +258,111 @@ def tile_causalshapedattention_pa_t_kernel(tc, q, k, v, alpha, beta, gamma, out)
                 in1=diag_add[:, i, :], op0=ALU.mult, op1=ALU.add,
             )
 
-        def transpose_shaped(unit):
-            if not live(unit):
+        def transpose_shaped(r):
+            if not live(r):
                 return
-            words = shaped_tiles[unit % NT][:].bitcast(F32)
-            pt_ps = ps_pt.tile([P, 2, P], F32, tag="pt")
-            for u in range(2):
-                nc.tensor.transpose(pt_ps[:, u, :], words[:, u * P : (u + 1) * P], ident_f32[:])
-            pt_banks[unit] = pt_ps
+            pt_ps = ps_pt.tile([P, 2, 2, P], F32, tag="pt")
+            for m in range(2):
+                words = shaped_tiles[query_tiles(r)[m]][:].bitcast(F32)
+                for u in range(2):
+                    nc.tensor.transpose(pt_ps[:, m, u, :], words[:, u * P : (u + 1) * P], ident_f32[:])
+            pt_banks[r] = pt_ps
 
-        def group_shaped(unit):
-            if not live(unit):
+        def group_shaped(r):
+            if not live(r):
                 return
-            grouped = rows.tile([P, P, PACK], BF16, tag="grouped", align_bytes=64)
+            grouped = pairs.tile([P, 2, P, PACK], BF16, tag="grouped", align_bytes=64)
             nc.vector.tensor_copy(
-                out=grouped[:].rearrange("p r t -> p (r t)").bitcast(F32).rearrange("p (r u) -> p r u", u=2),
-                in_=pt_banks[unit][:].rearrange("p u r -> p r u"),
+                out=grouped[:].rearrange("p m r t -> p (m r t)").bitcast(F32).rearrange("p (m r u) -> p m r u", m=2, u=2),
+                in_=pt_banks[r][:].rearrange("p m u r -> p m r u"),
             )
-            groupeds[unit] = grouped
+            groupeds[r] = grouped
 
-        def quantise_shaped(unit):
-            if not live(unit):
+        def quantise_shaped(r):
+            if not live(r):
                 return
-            p_codes = rows.tile([P, P], U32, tag="p_codes", align_bytes=64)
-            p_scales = rows.tile([P, P], U8, tag="p_scales", align_bytes=64)
+            p_codes = pairs.tile([P, 2 * P], U32, tag="p_codes", align_bytes=64)
+            p_scales = pairs.tile([P, 2 * P], U8, tag="p_scales", align_bytes=64)
             nc.vector.quantize_mx(
                 out=p_codes[:].bitcast(FP8X4), scales=p_scales[:],
-                in_=groupeds[unit][:].rearrange("p r t -> p (r t)"),
+                in_=groupeds[r][:].rearrange("p m r t -> p (m r t)"),
             )
-            p_words[unit] = (p_codes, p_scales)
+            p_words[r] = (p_codes, p_scales)
 
-        def group_values(unit):
-            if not live(unit):
+        def group_values(r):
+            if not live(r):
                 return
-            n, piece = divmod(unit, NT)
-            v_grouped = rows.tile([P, P, PACK], BF16, tag="v_grouped", align_bytes=64)
+            n, piece = divmod(r, 2)
+            v_grouped = pairs.tile([P, HALF, PACK], BF16, tag="v_grouped", align_bytes=64)
             nc.vector.tensor_copy(
                 out=v_grouped[:].rearrange("p (c i) t -> p c t i", i=4),
-                in_=v_tiles[n][:, :, piece * P : (piece + 1) * P].rearrange("p t (c i) -> p c t i", i=4),
+                in_=v_sbs[n][:, :, piece * HALF : (piece + 1) * HALF].rearrange("p t (c i) -> p c t i", i=4),
             )
-            v_groupeds[unit] = v_grouped
+            v_groupeds[r] = v_grouped
 
-        def quantise_values(unit):
-            if not live(unit):
+        def quantise_values(r):
+            if not live(r):
                 return
-            n, piece = divmod(unit, NT)
+            n, piece = divmod(r, 2)
             if piece == 0:
                 v_codes = seqs.tile([P, C], U32, tag="v_codes", align_bytes=64)
                 v_scales = seqs.tile([P, C], U8, tag="v_scales", align_bytes=64)
                 v_words[n] = (v_codes, v_scales)
             v_codes, v_scales = v_words[n]
-            cols = slice(piece * P, (piece + 1) * P)
+            cols = slice(piece * HALF, (piece + 1) * HALF)
             nc.vector.quantize_mx(
                 out=v_codes[:, cols].bitcast(FP8X4), scales=v_scales[:, cols],
-                in_=v_groupeds[unit][:].rearrange("p c t -> p (c t)"),
+                in_=v_groupeds[r][:].rearrange("p c t -> p (c t)"),
             )
 
-        def multiply_values(unit):
-            if not live(unit):
+        def multiply_values(r):
+            if not live(r):
                 return
-            n = unit // NT
-            p_codes, p_scales = p_words[unit]
-            v_codes, v_scales = v_words[n]
-            o_ps = ps_o.tile([P, C], F32, tag="o")
-            nc.tensor.matmul_mx(
-                out=o_ps[:],
-                lhsT=p_codes[:].bitcast(FP8X4), lhsT_scale=p_scales[:],
-                rhs=v_codes[:].bitcast(FP8X4), rhs_scale=v_scales[:],
-                start=True, stop=True,
-            )
-            o_banks[unit] = o_ps
+            p_codes, p_scales = p_words[r]
+            v_codes, v_scales = v_words[r // 2]
+            for m in range(2):
+                queries = slice(m * P, (m + 1) * P)
+                o_ps = ps_o.tile([P, C], F32, tag="o")
+                nc.tensor.matmul_mx(
+                    out=o_ps[:],
+                    lhsT=p_codes[:, queries].bitcast(FP8X4), lhsT_scale=p_scales[:, queries],
+                    rhs=v_codes[:].bitcast(FP8X4), rhs_scale=v_scales[:],
+                    start=True, stop=True,
+                )
+                o_banks[r, m] = o_ps
 
-        def store_output(unit):
-            if not live(unit):
+        def store_output(r, m):
+            if not live(r):
                 return
-            n, i = divmod(unit, NT)
+            n, i = r // 2, query_tiles(r)[m]
             o_sb = stores.tile([P, C], F32, tag="o_sb")
-            nc.scalar.copy(out=o_sb[:], in_=o_banks[unit][:])
+            if (r, m) == (ROUNDS - 1, 1):
+                nc.vector.tensor_copy(out=o_sb[:], in_=o_banks[r, m][:])
+            else:
+                nc.scalar.copy(out=o_sb[:], in_=o_banks[r, m][:])
             nc.sync.dma_start(out=out[n, i * P : (i + 1) * P, :], in_=o_sb[:])
 
-        for tick in range(-2, UNITS + 6):
-            store_output(tick - 5)
-            copy_transposed_inputs(tick + 1)
-            row_max(tick - 1)
-            invert_sum(tick - 2)
-            row_shift(tick - 1)
-            row_gain(tick - 2)
-            exponentials(tick - 1)
-            transpose_shaped(tick - 3)
-            group_shaped(tick - 3)
-            group_values(tick)
-            shape_rows(tick - 2)
-            quantise_shaped(tick - 3)
-            quantise_values(tick)
-            scores(tick, (0, 1))
-            multiply_values(tick - 4)
-            scores(tick, (2, 3))
-            transpose_inputs(tick + 2)
+        for r in range(-2, ROUNDS + 2):
+            transpose_shaped(r - 2)
+            scale_and_shift(r - 1, 1)
+            exponentials(r - 1, 1)
+            row_gain(r - 1, 1)
+            group_shaped(r - 2)
+            scores(r, 0, (0, 1, 2, 3))
+            transpose_inputs(2 * r + 3)
+            transpose_inputs(2 * r + 4)
+            copy_transposed_inputs(2 * r + 3)
+            copy_transposed_inputs(2 * r + 4)
+            quantise_values(r - 1)
+            quantise_shaped(r - 2)
+            scale_and_shift(r, 0)
+            exponentials(r, 0)
+            row_gain(r, 0)
+            scores(r, 1, (0, 1))
+            multiply_values(r - 2)
+            scores(r, 1, (2, 3))
+            store_output(r - 2, 0)
+            store_output(r - 2, 1)
+            group_values(r)
+            shape_rows(r - 1, 0)
+            shape_rows(r - 1, 1)

@@ -123,7 +123,7 @@ def tile_causalshapedattention_pa_t_kernel(tc, q, k, v, alpha, beta, gamma, out)
         nc.vector.tensor_copy(out=row_number[:], in_=row_number_i[:])
         mean_weight = consts.tile([P, NT], F32)
         nc.vector.reciprocal(out=mean_weight[:], in_=row_number[:])
-        minus_one = consts.tile([P, 1], F32)
+        minus_one = consts.tile([P, 2], F32)
         nc.gpsimd.memset(minus_one[:], -1.0)
 
         shaped_tiles = []
@@ -134,8 +134,9 @@ def tile_causalshapedattention_pa_t_kernel(tc, q, k, v, alpha, beta, gamma, out)
 
         alpha_f = consts.tile([P, 1], F32)
         nc.vector.tensor_copy(out=alpha_f[:], in_=alpha_bf[:])
-        beta_f = consts.tile([P, 1], F32)
-        nc.vector.tensor_copy(out=beta_f[:], in_=beta_bf[:])
+        beta_pair = consts.tile([P, 2], F32)
+        for m in range(2):
+            nc.vector.tensor_copy(out=beta_pair[:, m : m + 1], in_=beta_bf[:])
         gamma_f = consts.tile([P, 1], F32)
         nc.vector.tensor_copy(out=gamma_f[:], in_=gamma_bf[:])
 
@@ -224,37 +225,39 @@ def tile_causalshapedattention_pa_t_kernel(tc, q, k, v, alpha, beta, gamma, out)
                 return
             keys = (query_tiles(r)[m] + 1) * P
             e_sb = rows.tile([P, T], F32, tag="e")
-            e_sum = rows.tile([P, 1], F32, tag="e_sum")
+            if m == 0:
+                e_sum = pairs.tile([P, 2], F32, tag="e_sum")
+                e_sums[r] = e_sum
             nc.scalar.activation(
                 out=e_sb[:, :keys], in_=neg_scores[r, m][:, :keys], func=ACT.Exp,
-                bias=shifts[r, m][:, 0:1], scale=-1.0, accum_out=e_sum[:],
+                bias=shifts[r, m][:, 0:1], scale=-1.0, accum_out=e_sums[r][:, m : m + 1],
             )
-            e_tiles[r, m], e_sums[r, m] = e_sb, e_sum
+            e_tiles[r, m] = e_sb
 
-        def row_gain(r, m):
+        def row_gain(r):
             if not live(r):
                 return
-            inv_sum = rows.tile([P, 1], F32, tag="inv_sum")
-            nc.gpsimd.tensor_tensor(out=inv_sum[:], in0=e_sums[r, m][:], in1=minus_one[:], op=ALU.pow)
-            gain = rows.tile([P, 1], F32, tag="gain")
-            nc.gpsimd.tensor_tensor(out=gain[:], in0=inv_sum[:], in1=beta_f[:], op=ALU.mult)
-            gains[r, m] = gain
+            inv_sum = pairs.tile([P, 2], F32, tag="inv_sum")
+            nc.gpsimd.tensor_tensor(out=inv_sum[:], in0=e_sums[r][:], in1=minus_one[:], op=ALU.pow)
+            gain = pairs.tile([P, 2], F32, tag="gain")
+            nc.gpsimd.tensor_tensor(out=gain[:], in0=inv_sum[:], in1=beta_pair[:], op=ALU.mult)
+            gains[r] = gain
 
         def shape_rows(r, m):
             if not live(r):
                 return
             i = query_tiles(r)[m]
             keys = (i + 1) * P
-            e_sb, gain = e_tiles[r, m], gains[r, m]
+            e_sb, gain = e_tiles[r, m], gains[r][:, m : m + 1]
             shaped = shaped_tiles[i]
             if i > 0:
                 nc.vector.tensor_scalar(
                     out=shaped[:, : i * P], in0=e_sb[:, : i * P],
-                    scalar1=gain[:, 0:1], scalar2=neg_mc[:, i : i + 1],
+                    scalar1=gain, scalar2=neg_mc[:, i : i + 1],
                     op0=ALU.mult, op1=ALU.add,
                 )
             nc.vector.scalar_tensor_tensor(
-                out=shaped[:, i * P : keys], in0=e_sb[:, i * P : keys], scalar=gain[:, 0:1],
+                out=shaped[:, i * P : keys], in0=e_sb[:, i * P : keys], scalar=gain,
                 in1=diag_add[:, i, :], op0=ALU.mult, op1=ALU.add,
             )
 
@@ -342,27 +345,26 @@ def tile_causalshapedattention_pa_t_kernel(tc, q, k, v, alpha, beta, gamma, out)
                 nc.scalar.copy(out=o_sb[:], in_=o_banks[r, m][:])
             nc.sync.dma_start(out=out[n, i * P : (i + 1) * P, :], in_=o_sb[:])
 
-        for r in range(-2, ROUNDS + 2):
-            transpose_shaped(r - 2)
-            scale_and_shift(r - 1, 1)
-            exponentials(r - 1, 1)
-            row_gain(r - 1, 1)
-            group_shaped(r - 2)
-            scores(r, 0, (0, 1, 2, 3))
+        for r in range(-2, ROUNDS + 4):
             transpose_inputs(2 * r + 3)
             transpose_inputs(2 * r + 4)
+            scale_and_shift(r - 1, 1)
+            quantise_shaped(r - 4)
+            quantise_values(r - 1)
             copy_transposed_inputs(2 * r + 3)
             copy_transposed_inputs(2 * r + 4)
-            quantise_values(r - 1)
-            quantise_shaped(r - 2)
+            exponentials(r - 1, 1)
+            row_gain(r - 1)
+            scores(r, 0, (0, 1, 2, 3))
             scale_and_shift(r, 0)
             exponentials(r, 0)
-            row_gain(r, 0)
-            scores(r, 1, (0, 1))
-            multiply_values(r - 2)
-            scores(r, 1, (2, 3))
-            store_output(r - 2, 0)
-            store_output(r - 2, 1)
+            transpose_shaped(r - 3)
             group_values(r)
-            shape_rows(r - 1, 0)
-            shape_rows(r - 1, 1)
+            group_shaped(r - 3)
+            scores(r, 1, (0, 1))
+            multiply_values(r - 4)
+            scores(r, 1, (2, 3))
+            store_output(r - 4, 0)
+            store_output(r - 4, 1)
+            shape_rows(r - 2, 0)
+            shape_rows(r - 2, 1)

@@ -20,6 +20,7 @@ PACK = 4
 ROUNDS = 2 * B
 BANKS = 4 * B
 HALF = C // 2
+SPREAD = 16
 SCALE = 1.0 / math.sqrt(C)
 MASKED = -1.0e30
 
@@ -53,12 +54,12 @@ def tile_causalshapedattention_pa_t_kernel(tc, q, k, v, alpha, beta, gamma, out)
         ps_o = ctx.enter_context(tc.psum_pool(name="ps_o", bufs=2))
         ctx.enter_context(tc.manual_schedule())
 
-        alpha_bf = consts.tile([P, 1], BF16)
-        nc.scalar.dma_start(out=alpha_bf[:], in_=alpha.partition_broadcast(P))
-        beta_bf = consts.tile([P, 1], BF16)
-        nc.scalar.dma_start(out=beta_bf[:], in_=beta.partition_broadcast(P))
-        gamma_bf = consts.tile([P, 1], BF16)
-        nc.scalar.dma_start(out=gamma_bf[:], in_=gamma.partition_broadcast(P))
+        scalars_row = consts.tile([P, 4 * SPREAD], BF16)
+        nc.vector.memset(scalars_row[:], 0.0)
+        for j, scalar in enumerate((alpha, beta, gamma)):
+            nc.scalar.dma_start(out=scalars_row[0:1, j * SPREAD : j * SPREAD + 1], in_=scalar.unsqueeze(0))
+        ones = consts.tile([P, P], BF16)
+        nc.vector.memset(ones[:], 1.0)
 
         warm = consts.tile([P, 1], F32)
         nc.vector.memset(warm[:], 0.0)
@@ -86,19 +87,18 @@ def tile_causalshapedattention_pa_t_kernel(tc, q, k, v, alpha, beta, gamma, out)
                 in_=v[n].rearrange("(u p e) c -> p u (e c)", p=P, e=2),
             )
 
-        for n in range(2):
+        for n in range(B):
             load_tokens("k", n, 0, 2)
-            if n == 1:
-                load_values(0)
+            if n > 0:
+                load_values(n - 1)
             load_tokens("k", n, 2, 2)
-            load_tokens("q", n, 0, 1)
-            load_tokens("q", n, 3, 1)
-            load_tokens("q", n, 1, 2)
-        load_values(1)
-        for n in range(2, B):
-            load_tokens("k", n, 0, NT)
-            load_tokens("q", n, 0, NT)
-            load_values(n)
+            if n < 2:
+                load_tokens("q", n, 0, 1)
+                load_tokens("q", n, 3, 1)
+                load_tokens("q", n, 1, 2)
+            else:
+                load_tokens("q", n, 0, NT)
+        load_values(B - 1)
 
         ident_f32 = consts.tile([P, P], F32)
         make_identity(nc, ident_f32[:])
@@ -132,22 +132,25 @@ def tile_causalshapedattention_pa_t_kernel(tc, q, k, v, alpha, beta, gamma, out)
             nc.vector.memset(shaped[:], 0.0)
             shaped_tiles.append(shaped)
 
-        alpha_f = consts.tile([P, 1], F32)
-        nc.vector.tensor_copy(out=alpha_f[:], in_=alpha_bf[:])
+        scalars_ps = ps_o.tile([P, C], F32, tag="o")
+        nc.tensor.matmul(scalars_ps[:, : 4 * SPREAD], lhsT=ones[:], rhs=scalars_row[:], start=True, stop=True)
+        scalars_f = consts.tile([P, 4 * SPREAD], F32)
+        nc.vector.tensor_copy(out=scalars_f[:], in_=scalars_ps[:, : 4 * SPREAD])
+        alpha_f = scalars_f[:, 0:1]
+        beta_f = scalars_f[:, SPREAD : SPREAD + 1]
+        gamma_f = scalars_f[:, 2 * SPREAD : 2 * SPREAD + 1]
         beta_pair = consts.tile([P, 2], F32)
         for m in range(2):
-            nc.vector.tensor_copy(out=beta_pair[:, m : m + 1], in_=beta_bf[:])
-        gamma_f = consts.tile([P, 1], F32)
-        nc.vector.tensor_copy(out=gamma_f[:], in_=gamma_bf[:])
+            nc.vector.tensor_copy(out=beta_pair[:, m : m + 1], in_=beta_f)
 
         neg_mc = consts.tile([P, NT], F32)
         nc.vector.tensor_scalar(
-            out=neg_mc[:], in0=mean_weight[:], scalar1=gamma_f[:, 0:1], scalar2=-1.0,
+            out=neg_mc[:], in0=mean_weight[:], scalar1=gamma_f, scalar2=-1.0,
             op0=ALU.mult, op1=ALU.mult,
         )
         alpha_eye = consts.tile([P, P], F32)
         nc.vector.tensor_scalar(
-            out=alpha_eye[:], in0=ident_f32[:], scalar1=alpha_f[:, 0:1], scalar2=None,
+            out=alpha_eye[:], in0=ident_f32[:], scalar1=alpha_f, scalar2=None,
             op0=ALU.mult,
         )
         diag_add = consts.tile([P, NT, P], F32)

@@ -19,8 +19,7 @@ NT = T // P
 PACK = 4
 ROUNDS = 2 * B
 BANKS = 4 * B
-HALF = C // 2
-SPREAD = 16
+V_CHUNK = C // 2
 SCALE = 1.0 / math.sqrt(C)
 MASKED = -1.0e30
 
@@ -44,9 +43,9 @@ def tile_causalshapedattention_pa_t_kernel(tc, q, k, v, alpha, beta, gamma, out)
     with ExitStack() as ctx:
         consts = ctx.enter_context(tc.tile_pool(name="consts", bufs=1))
         loads = ctx.enter_context(tc.tile_pool(name="loads", bufs=B))
-        seqs = ctx.enter_context(tc.tile_pool(name="seqs", bufs=3))
-        rows = ctx.enter_context(tc.tile_pool(name="rows", bufs=6))
-        pairs = ctx.enter_context(tc.tile_pool(name="pairs", bufs=3))
+        per_seq = ctx.enter_context(tc.tile_pool(name="per_seq", bufs=3))
+        per_tile = ctx.enter_context(tc.tile_pool(name="per_tile", bufs=6))
+        per_round = ctx.enter_context(tc.tile_pool(name="per_round", bufs=3))
         stores = ctx.enter_context(tc.tile_pool(name="stores", bufs=16))
         ps_tr = ctx.enter_context(tc.psum_pool(name="ps_tr", bufs=2))
         ps_s = ctx.enter_context(tc.psum_pool(name="ps_s", bufs=3))
@@ -54,12 +53,12 @@ def tile_causalshapedattention_pa_t_kernel(tc, q, k, v, alpha, beta, gamma, out)
         ps_o = ctx.enter_context(tc.psum_pool(name="ps_o", bufs=2))
         ctx.enter_context(tc.manual_schedule())
 
-        scalars_row = consts.tile([P, 4 * SPREAD], BF16)
-        nc.vector.memset(scalars_row[:], 0.0)
-        for j, scalar in enumerate((alpha, beta, gamma)):
-            nc.scalar.dma_start(out=scalars_row[0:1, j * SPREAD : j * SPREAD + 1], in_=scalar.unsqueeze(0))
-        ones = consts.tile([P, P], BF16)
-        nc.vector.memset(ones[:], 1.0)
+        alpha_bf = consts.tile([P, 1], BF16)
+        nc.scalar.dma_start(out=alpha_bf[:], in_=alpha.partition_broadcast(P))
+        beta_bf = consts.tile([P, 1], BF16)
+        nc.scalar.dma_start(out=beta_bf[:], in_=beta.partition_broadcast(P))
+        gamma_bf = consts.tile([P, 1], BF16)
+        nc.scalar.dma_start(out=gamma_bf[:], in_=gamma.partition_broadcast(P))
 
         warm = consts.tile([P, 1], F32)
         nc.vector.memset(warm[:], 0.0)
@@ -132,25 +131,22 @@ def tile_causalshapedattention_pa_t_kernel(tc, q, k, v, alpha, beta, gamma, out)
             nc.vector.memset(shaped[:], 0.0)
             shaped_tiles.append(shaped)
 
-        scalars_ps = ps_o.tile([P, C], F32, tag="o")
-        nc.tensor.matmul(scalars_ps[:, : 4 * SPREAD], lhsT=ones[:], rhs=scalars_row[:], start=True, stop=True)
-        scalars_f = consts.tile([P, 4 * SPREAD], F32)
-        nc.vector.tensor_copy(out=scalars_f[:], in_=scalars_ps[:, : 4 * SPREAD])
-        alpha_f = scalars_f[:, 0:1]
-        beta_f = scalars_f[:, SPREAD : SPREAD + 1]
-        gamma_f = scalars_f[:, 2 * SPREAD : 2 * SPREAD + 1]
+        alpha_f = consts.tile([P, 1], F32)
+        nc.vector.tensor_copy(out=alpha_f[:], in_=alpha_bf[:])
         beta_pair = consts.tile([P, 2], F32)
         for m in range(2):
-            nc.vector.tensor_copy(out=beta_pair[:, m : m + 1], in_=beta_f)
+            nc.vector.tensor_copy(out=beta_pair[:, m : m + 1], in_=beta_bf[:])
+        gamma_f = consts.tile([P, 1], F32)
+        nc.vector.tensor_copy(out=gamma_f[:], in_=gamma_bf[:])
 
         neg_mc = consts.tile([P, NT], F32)
         nc.vector.tensor_scalar(
-            out=neg_mc[:], in0=mean_weight[:], scalar1=gamma_f, scalar2=-1.0,
+            out=neg_mc[:], in0=mean_weight[:], scalar1=gamma_f[:, 0:1], scalar2=-1.0,
             op0=ALU.mult, op1=ALU.mult,
         )
         alpha_eye = consts.tile([P, P], F32)
         nc.vector.tensor_scalar(
-            out=alpha_eye[:], in0=ident_f32[:], scalar1=alpha_f, scalar2=None,
+            out=alpha_eye[:], in0=ident_f32[:], scalar1=alpha_f[:, 0:1], scalar2=None,
             op0=ALU.mult,
         )
         diag_add = consts.tile([P, NT, P], F32)
@@ -170,11 +166,11 @@ def tile_causalshapedattention_pa_t_kernel(tc, q, k, v, alpha, beta, gamma, out)
             if not 0 <= bank < BANKS:
                 return
             name, n, half, tiles = bank_contents(bank)
-            words = x_sbs[name, n][:].bitcast(F32)
+            as_f32 = x_sbs[name, n][:].bitcast(F32)
             tr = ps_tr.tile([P, 2, 2, P], F32, tag="tr")
             for m in range(2):
                 for u in range(2):
-                    nc.tensor.transpose(tr[:, m, u, :], words[:, tiles[m], u * P : (u + 1) * P], ident_f32[:])
+                    nc.tensor.transpose(tr[:, m, u, :], as_f32[:, tiles[m], u * P : (u + 1) * P], ident_f32[:])
             tr_banks[bank] = tr
 
         def copy_transposed_inputs(bank):
@@ -182,7 +178,7 @@ def tile_causalshapedattention_pa_t_kernel(tc, q, k, v, alpha, beta, gamma, out)
                 return
             name, n, half, tiles = bank_contents(bank)
             if half == 0:
-                x_t = seqs.tile([P, NT, 2, P, 2], BF16, tag=name + "_t")
+                x_t = per_seq.tile([P, NT, 2, P, 2], BF16, tag=name + "_t")
                 x_ts[name, n] = x_t
             nc.scalar.copy(
                 out=x_ts[name, n][:, 2 * half : 2 * half + 2, :, :, :].rearrange("p m u t e -> p (m u t e)"),
@@ -215,8 +211,8 @@ def tile_causalshapedattention_pa_t_kernel(tc, q, k, v, alpha, beta, gamma, out)
             if not live(r):
                 return
             keys = (query_tiles(r)[m] + 1) * P
-            neg_s = rows.tile([P, T], F32, tag="neg_s")
-            shift = rows.tile([P, 1], F32, tag="shift")
+            neg_s = per_tile.tile([P, T], F32, tag="neg_s")
+            shift = per_tile.tile([P, 1], F32, tag="shift")
             nc.vector.tensor_scalar(
                 out=neg_s[:, :keys], in0=s_banks[r, m][:, :keys], scalar1=-SCALE, scalar2=None,
                 op0=ALU.mult, op1=ALU.min, accum_out=shift[:],
@@ -227,9 +223,9 @@ def tile_causalshapedattention_pa_t_kernel(tc, q, k, v, alpha, beta, gamma, out)
             if not live(r):
                 return
             keys = (query_tiles(r)[m] + 1) * P
-            e_sb = rows.tile([P, T], F32, tag="e")
+            e_sb = per_tile.tile([P, T], F32, tag="e")
             if m == 0:
-                e_sum = pairs.tile([P, 2], F32, tag="e_sum")
+                e_sum = per_round.tile([P, 2], F32, tag="e_sum")
                 e_sums[r] = e_sum
             nc.scalar.activation(
                 out=e_sb[:, :keys], in_=neg_scores[r, m][:, :keys], func=ACT.Exp,
@@ -240,9 +236,9 @@ def tile_causalshapedattention_pa_t_kernel(tc, q, k, v, alpha, beta, gamma, out)
         def row_gain(r):
             if not live(r):
                 return
-            inv_sum = pairs.tile([P, 2], F32, tag="inv_sum")
+            inv_sum = per_round.tile([P, 2], F32, tag="inv_sum")
             nc.gpsimd.tensor_tensor(out=inv_sum[:], in0=e_sums[r][:], in1=minus_one[:], op=ALU.pow)
-            gain = pairs.tile([P, 2], F32, tag="gain")
+            gain = per_round.tile([P, 2], F32, tag="gain")
             nc.gpsimd.tensor_tensor(out=gain[:], in0=inv_sum[:], in1=beta_pair[:], op=ALU.mult)
             gains[r] = gain
 
@@ -269,53 +265,53 @@ def tile_causalshapedattention_pa_t_kernel(tc, q, k, v, alpha, beta, gamma, out)
                 return
             pt_ps = ps_pt.tile([P, 2, 2, P], F32, tag="pt")
             for m in range(2):
-                words = shaped_tiles[query_tiles(r)[m]][:].bitcast(F32)
+                as_f32 = shaped_tiles[query_tiles(r)[m]][:].bitcast(F32)
                 for u in range(2):
-                    nc.tensor.transpose(pt_ps[:, m, u, :], words[:, u * P : (u + 1) * P], ident_f32[:])
+                    nc.tensor.transpose(pt_ps[:, m, u, :], as_f32[:, u * P : (u + 1) * P], ident_f32[:])
             pt_banks[r] = pt_ps
 
         def group_shaped(r):
             if not live(r):
                 return
-            grouped = pairs.tile([P, 2, P, PACK], BF16, tag="grouped", align_bytes=64)
+            grouped = per_round.tile([P, 2, P, PACK], BF16, tag="grouped", align_bytes=64)
             nc.vector.tensor_copy(
-                out=grouped[:].rearrange("p m r t -> p (m r t)").bitcast(F32).rearrange("p (m r u) -> p m r u", m=2, u=2),
-                in_=pt_banks[r][:].rearrange("p m u r -> p m r u"),
+                out=grouped[:].rearrange("p m x t -> p (m x t)").bitcast(F32).rearrange("p (m x u) -> p m x u", m=2, u=2),
+                in_=pt_banks[r][:].rearrange("p m u x -> p m x u"),
             )
             groupeds[r] = grouped
 
         def quantise_shaped(r):
             if not live(r):
                 return
-            p_codes = pairs.tile([P, 2 * P], U32, tag="p_codes", align_bytes=64)
-            p_scales = pairs.tile([P, 2 * P], U8, tag="p_scales", align_bytes=64)
+            p_codes = per_round.tile([P, 2 * P], U32, tag="p_codes", align_bytes=64)
+            p_scales = per_round.tile([P, 2 * P], U8, tag="p_scales", align_bytes=64)
             nc.vector.quantize_mx(
                 out=p_codes[:].bitcast(FP8X4), scales=p_scales[:],
-                in_=groupeds[r][:].rearrange("p m r t -> p (m r t)"),
+                in_=groupeds[r][:].rearrange("p m x t -> p (m x t)"),
             )
             p_words[r] = (p_codes, p_scales)
 
         def group_values(r):
             if not live(r):
                 return
-            n, piece = divmod(r, 2)
-            v_grouped = pairs.tile([P, HALF, PACK], BF16, tag="v_grouped", align_bytes=64)
+            n, chunk = divmod(r, 2)
+            v_grouped = per_round.tile([P, V_CHUNK, PACK], BF16, tag="v_grouped", align_bytes=64)
             nc.vector.tensor_copy(
                 out=v_grouped[:].rearrange("p (c i) t -> p c t i", i=4),
-                in_=v_sbs[n][:, :, piece * HALF : (piece + 1) * HALF].rearrange("p t (c i) -> p c t i", i=4),
+                in_=v_sbs[n][:, :, chunk * V_CHUNK : (chunk + 1) * V_CHUNK].rearrange("p t (c i) -> p c t i", i=4),
             )
             v_groupeds[r] = v_grouped
 
         def quantise_values(r):
             if not live(r):
                 return
-            n, piece = divmod(r, 2)
-            if piece == 0:
-                v_codes = seqs.tile([P, C], U32, tag="v_codes", align_bytes=64)
-                v_scales = seqs.tile([P, C], U8, tag="v_scales", align_bytes=64)
+            n, chunk = divmod(r, 2)
+            if chunk == 0:
+                v_codes = per_seq.tile([P, C], U32, tag="v_codes", align_bytes=64)
+                v_scales = per_seq.tile([P, C], U8, tag="v_scales", align_bytes=64)
                 v_words[n] = (v_codes, v_scales)
             v_codes, v_scales = v_words[n]
-            cols = slice(piece * HALF, (piece + 1) * HALF)
+            cols = slice(chunk * V_CHUNK, (chunk + 1) * V_CHUNK)
             nc.vector.quantize_mx(
                 out=v_codes[:, cols].bitcast(FP8X4), scales=v_scales[:, cols],
                 in_=v_groupeds[r][:].rearrange("p c t -> p (c t)"),
@@ -348,7 +344,7 @@ def tile_causalshapedattention_pa_t_kernel(tc, q, k, v, alpha, beta, gamma, out)
                 nc.scalar.copy(out=o_sb[:], in_=o_banks[r, m][:])
             nc.sync.dma_start(out=out[n, i * P : (i + 1) * P, :], in_=o_sb[:])
 
-        for r in range(-2, ROUNDS + 4):
+        def turn(r):
             transpose_inputs(2 * r + 3)
             transpose_inputs(2 * r + 4)
             scale_and_shift(r - 1, 1)
@@ -371,3 +367,6 @@ def tile_causalshapedattention_pa_t_kernel(tc, q, k, v, alpha, beta, gamma, out)
             store_output(r - 4, 1)
             shape_rows(r - 2, 0)
             shape_rows(r - 2, 1)
+
+        for r in range(-2, ROUNDS + 4):
+            turn(r)

@@ -181,8 +181,8 @@ def tile_causalshapedattention_pa_t_kernel(tc, q, k, v, alpha, beta, gamma, out)
                 x_t = per_seq.tile([P, NT, 2, P, 2], BF16, tag=name + "_t")
                 x_ts[name, n] = x_t
             nc.scalar.copy(
-                out=x_ts[name, n][:, 2 * half : 2 * half + 2, :, :, :].rearrange("p m u t e -> p (m u t e)"),
-                in_=tr_banks[bank][:].rearrange("p m u t -> p (m u t)").bitcast(BF16),
+                out=x_ts[name, n][:, 2 * half : 2 * half + 2, :, :, :].rearrange("p m u t e -> p (m u t e)").bitcast(F32),
+                in_=tr_banks[bank][:].rearrange("p m u t -> p (m u t)"),
             )
 
         def scores(r, m, steps):
@@ -274,10 +274,12 @@ def tile_causalshapedattention_pa_t_kernel(tc, q, k, v, alpha, beta, gamma, out)
             if not live(r):
                 return
             grouped = per_round.tile([P, 2, P, PACK], BF16, tag="grouped", align_bytes=64)
-            nc.vector.tensor_copy(
-                out=grouped[:].rearrange("p m x t -> p (m x t)").bitcast(F32).rearrange("p (m x u) -> p m x u", m=2, u=2),
-                in_=pt_banks[r][:].rearrange("p m u x -> p m x u"),
-            )
+            words_out = grouped[:].rearrange("p m x t -> p (m x t)").bitcast(F32).rearrange("p (m x u) -> p m x u", m=2, u=2)
+            words_in = pt_banks[r][:].rearrange("p m u x -> p m x u")
+            if r % 4 == 3 or r >= ROUNDS - 4:
+                nc.scalar.copy(out=words_out, in_=words_in)
+            else:
+                nc.vector.tensor_copy(out=words_out, in_=words_in)
             groupeds[r] = grouped
 
         def quantise_shaped(r):

@@ -159,6 +159,8 @@ def tile_causalshapedattention_pa_t_kernel(tc, q, k, v, alpha, beta, gamma, out)
         tr_banks, x_ts, s_banks, neg_scores, shifts, e_tiles, e_sums, gains = {}, {}, {}, {}, {}, {}, {}, {}
         pt_banks, groupeds, p_words, v_groupeds, v_words, o_banks = {}, {}, {}, {}, {}, {}
 
+        pt_ps = ps_pt.tile([P, 2, 2, P], F32)
+
         def live(r):
             return 0 <= r < ROUNDS
 
@@ -263,10 +265,11 @@ def tile_causalshapedattention_pa_t_kernel(tc, q, k, v, alpha, beta, gamma, out)
         def transpose_shaped(r):
             if not live(r):
                 return
-            pt_ps = ps_pt.tile([P, 2, 2, P], F32, tag="pt")
             for m in range(2):
                 as_f32 = shaped_tiles[query_tiles(r)[m]][:].bitcast(F32)
                 for u in range(2):
+                    if (m, u) == (0, 1) and r > 0:
+                        continue
                     nc.tensor.transpose(pt_ps[:, m, u, :], as_f32[:, u * P : (u + 1) * P], ident_f32[:])
             pt_banks[r] = pt_ps
 

@@ -60,6 +60,9 @@ def tile_causalshapedattention_pa_t_kernel(tc, q, k, v, alpha, beta, gamma, out)
         gamma_bf = consts.tile([P, 1], BF16)
         nc.scalar.dma_start(out=gamma_bf[:], in_=gamma.partition_broadcast(P))
 
+        zeros = consts.tile([P, C], BF16)
+        nc.vector.memset(zeros[:], 0.0)
+
         warm = consts.tile([P, 1], F32)
         nc.vector.memset(warm[:], 0.0)
         warm_exp = consts.tile([P, 1], F32)
@@ -349,9 +352,18 @@ def tile_causalshapedattention_pa_t_kernel(tc, q, k, v, alpha, beta, gamma, out)
                 nc.scalar.copy(out=o_sb[:], in_=o_banks[r, m][:])
             nc.sync.dma_start(out=out[n, i * P : (i + 1) * P, :], in_=o_sb[:])
 
+        def keep_warm(count):
+            idle_ps = ps_o.tile([P, C], F32, tag="o")
+            for step in range(count):
+                nc.tensor.matmul(idle_ps[:], lhsT=zeros[:, :P], rhs=zeros[:], start=True, stop=True)
+
         def turn(r):
             transpose_inputs(2 * r + 3)
+            if -2 < r < 1:
+                keep_warm(1)
             transpose_inputs(2 * r + 4)
+            if r < 1:
+                keep_warm(1)
             scale_and_shift(r - 1, 1)
             quantise_shaped(r - 4)
             quantise_values(r - 1)
@@ -373,5 +385,6 @@ def tile_causalshapedattention_pa_t_kernel(tc, q, k, v, alpha, beta, gamma, out)
             shape_rows(r - 2, 0)
             shape_rows(r - 2, 1)
 
+        keep_warm(4)
         for r in range(-2, ROUNDS + 4):
             turn(r)

from contextlib import ExitStack
import math

import concourse.mybir as mybir
from concourse.masks import make_identity

F32 = mybir.dt.float32
BF16 = mybir.dt.bfloat16
I32 = mybir.dt.int32
U32 = mybir.dt.uint32
U8 = mybir.dt.uint8
FP8X4 = mybir.dt.float8_e4m3fn_x4
ALU = mybir.AluOpType
ACT = mybir.ActivationFunctionType

B, T, C = 8, 512, 512
P = 128
NT = T // P
PACK = 4
ROUNDS = 2 * B
BANKS = 4 * B
V_CHUNK = C // 2
SCALE = 1.0 / math.sqrt(C)
MASKED = -1.0e30

FLOPS = 2 * 2 * B * T * T * C


def query_tiles(r):
    first = r % 2
    return (first, NT - 1 - first)


def bank_contents(bank):
    n, j = divmod(bank, 4)
    if j < 2:
        return "k", n, j, (2 * j, 2 * j + 1)
    return "q", n, j - 2, query_tiles(j - 2)


def tile_causalshapedattention_pa_t_kernel(tc, q, k, v, alpha, beta, gamma, out):
    nc = tc.nc
    with ExitStack() as ctx:
        consts = ctx.enter_context(tc.tile_pool(name="consts", bufs=1))
        loads = ctx.enter_context(tc.tile_pool(name="loads", bufs=B))
        per_seq = ctx.enter_context(tc.tile_pool(name="per_seq", bufs=3))
        per_tile = ctx.enter_context(tc.tile_pool(name="per_tile", bufs=6))
        per_round = ctx.enter_context(tc.tile_pool(name="per_round", bufs=3))
        stores = ctx.enter_context(tc.tile_pool(name="stores", bufs=16))
        ps_tr = ctx.enter_context(tc.psum_pool(name="ps_tr", bufs=2))
        ps_s = ctx.enter_context(tc.psum_pool(name="ps_s", bufs=3))
        ps_pt = ctx.enter_context(tc.psum_pool(name="ps_pt", bufs=1))
        ps_o = ctx.enter_context(tc.psum_pool(name="ps_o", bufs=2))
        ctx.enter_context(tc.manual_schedule())

        alpha_bf = consts.tile([P, 1], BF16)
        nc.scalar.dma_start(out=alpha_bf[:], in_=alpha.partition_broadcast(P))
        beta_bf = consts.tile([P, 1], BF16)
        nc.scalar.dma_start(out=beta_bf[:], in_=beta.partition_broadcast(P))
        gamma_bf = consts.tile([P, 1], BF16)
        nc.scalar.dma_start(out=gamma_bf[:], in_=gamma.partition_broadcast(P))

        zeros = consts.tile([P, C], BF16)
        nc.vector.memset(zeros[:], 0.0)

        warm = consts.tile([P, 1], F32)
        nc.vector.memset(warm[:], 0.0)
        warm_exp = consts.tile([P, 1], F32)
        nc.scalar.activation(out=warm_exp[:], in_=warm[:], func=ACT.Exp)

        x_dram = {"k": k, "q": q}
        x_sbs, v_sbs = {}, {}
        for n in range(B):
            for name in ("k", "q"):
                x_sb = loads.tile([P, NT, C], BF16, tag=name)
                x_sbs[name, n] = x_sb
            v_sb = loads.tile([P, PACK, C], BF16, tag="v")
            v_sbs[n] = v_sb

        def load_tokens(name, n, first, count):
            nc.sync.dma_start(
                out=x_sbs[name, n][:, first : first + count, :],
                in_=x_dram[name][n, first * P : (first + count) * P, :].rearrange("(a p) c -> p a c", p=P),
            )

        def load_values(n):
            nc.sync.dma_start(
                out=v_sbs[n][:].rearrange("p (u e) c -> p u (e c)", e=2),
                in_=v[n].rearrange("(u p e) c -> p u (e c)", p=P, e=2),
            )

        for n in range(B):
            load_tokens("k", n, 0, 2)
            if n > 0:
                load_values(n - 1)
            load_tokens("k", n, 2, 2)
            if n < 2:
                load_tokens("q", n, 0, 1)
                load_tokens("q", n, 3, 1)
                load_tokens("q", n, 1, 2)
            else:
                load_tokens("q", n, 0, NT)
        load_values(B - 1)

        ident_f32 = consts.tile([P, P], F32)
        make_identity(nc, ident_f32[:])
        ident_bf = consts.tile([P, P], BF16)
        nc.vector.tensor_copy(out=ident_bf[:], in_=ident_f32[:])

        tril = consts.tile([P, P], F32)
        nc.gpsimd.memset(tril[:], 1.0)
        nc.gpsimd.affine_select(
            out=tril[:], in_=tril[:], compare_op=ALU.is_ge, fill=0.0,
            base=0, pattern=[[-1, P]], channel_multiplier=1,
        )
        mask_add = consts.tile([P, P], BF16)
        nc.vector.tensor_scalar(
            out=mask_add[:], in0=tril[:], scalar1=1.0, scalar2=-MASKED,
            op0=ALU.subtract, op1=ALU.mult,
        )

        row_number_i = consts.tile([P, NT], I32)
        nc.gpsimd.iota(row_number_i[:], pattern=[[P, NT]], base=1, channel_multiplier=1)
        row_number = consts.tile([P, NT], F32)
        nc.vector.tensor_copy(out=row_number[:], in_=row_number_i[:])
        mean_weight = consts.tile([P, NT], F32)
        nc.vector.reciprocal(out=mean_weight[:], in_=row_number[:])
        minus_one = consts.tile([P, 2], F32)
        nc.gpsimd.memset(minus_one[:], -1.0)

        shaped_tiles = []
        for i in range(NT):
            shaped = consts.tile([P, T], BF16, name="shaped%d" % i)
            nc.vector.memset(shaped[:], 0.0)
            shaped_tiles.append(shaped)

        alpha_f = consts.tile([P, 1], F32)
        nc.vector.tensor_copy(out=alpha_f[:], in_=alpha_bf[:])
        beta_pair = consts.tile([P, 2], F32)
        for m in range(2):
            nc.vector.tensor_copy(out=beta_pair[:, m : m + 1], in_=beta_bf[:])
        gamma_f = consts.tile([P, 1], F32)
        nc.vector.tensor_copy(out=gamma_f[:], in_=gamma_bf[:])

        neg_mc = consts.tile([P, NT], F32)
        nc.vector.tensor_scalar(
            out=neg_mc[:], in0=mean_weight[:], scalar1=gamma_f[:, 0:1], scalar2=-1.0,
            op0=ALU.mult, op1=ALU.mult,
        )
        alpha_eye = consts.tile([P, P], F32)
        nc.vector.tensor_scalar(
            out=alpha_eye[:], in0=ident_f32[:], scalar1=alpha_f[:, 0:1], scalar2=None,
            op0=ALU.mult,
        )
        diag_add = consts.tile([P, NT, P], F32)
        for i in range(NT):
            nc.vector.scalar_tensor_tensor(
                out=diag_add[:, i, :], in0=tril[:], scalar=neg_mc[:, i : i + 1],
                in1=alpha_eye[:], op0=ALU.mult, op1=ALU.add,
            )

        tr_banks, x_ts, s_banks, neg_scores, shifts, e_tiles, e_sums, gains = {}, {}, {}, {}, {}, {}, {}, {}
        pt_banks, groupeds, p_words, v_groupeds, v_words, o_banks = {}, {}, {}, {}, {}, {}

        pt_ps = ps_pt.tile([P, 2, 2, P], F32)

        def live(r):
            return 0 <= r < ROUNDS

        def transpose_inputs(bank):
            if not 0 <= bank < BANKS:
                return
            name, n, half, tiles = bank_contents(bank)
            as_f32 = x_sbs[name, n][:].bitcast(F32)
            tr = ps_tr.tile([P, 2, 2, P], F32, tag="tr")
            for m in range(2):
                for u in range(2):
                    nc.tensor.transpose(tr[:, m, u, :], as_f32[:, tiles[m], u * P : (u + 1) * P], ident_f32[:])
            tr_banks[bank] = tr

        def copy_transposed_inputs(bank):
            if not 0 <= bank < BANKS:
                return
            name, n, half, tiles = bank_contents(bank)
            if half == 0:
                x_t = per_seq.tile([P, NT, 2, P, 2], BF16, tag=name + "_t")
                x_ts[name, n] = x_t
            nc.scalar.copy(
                out=x_ts[name, n][:, 2 * half : 2 * half + 2, :, :, :].rearrange("p m u t e -> p (m u t e)").bitcast(F32),
                in_=tr_banks[bank][:].rearrange("p m u t -> p (m u t)"),
            )

        def scores(r, m, steps):
            if not live(r):
                return
            n, i = r // 2, query_tiles(r)[m]
            keys = (i + 1) * P
            if 0 in steps:
                s_ps = ps_s.tile([P, T], F32, tag="s")
                s_banks[r, m] = s_ps
            s_ps = s_banks[r, m]
            for step in steps:
                u, e = divmod(step, 2)
                nc.tensor.matmul(
                    s_ps[:, :keys].rearrange("p (a t) -> p a t", t=P),
                    lhsT=x_ts["q", n][:, 2 * (r % 2) + m, u, :, e], rhs=x_ts["k", n][:, : i + 1, u, :, e],
                    start=(step == 0), stop=(step == 3),
                )
                if step == 0:
                    nc.tensor.matmul(
                        s_ps[:, i * P : keys], lhsT=ident_bf[:], rhs=mask_add[:],
                        start=False, stop=False,
                    )

        def scale_and_shift(r, m):
            if not live(r):
                return
            keys = (query_tiles(r)[m] + 1) * P
            neg_s = per_tile.tile([P, T], F32, tag="neg_s")
            shift = per_tile.tile([P, 1], F32, tag="shift")
            nc.vector.tensor_scalar(
                out=neg_s[:, :keys], in0=s_banks[r, m][:, :keys], scalar1=-SCALE, scalar2=None,
                op0=ALU.mult, op1=ALU.min, accum_out=shift[:],
            )
            neg_scores[r, m], shifts[r, m] = neg_s, shift

        def exponentials(r, m):
            if not live(r):
                return
            keys = (query_tiles(r)[m] + 1) * P
            e_sb = per_tile.tile([P, T], F32, tag="e")
            if m == 0:
                e_sum = per_round.tile([P, 2], F32, tag="e_sum")
                e_sums[r] = e_sum
            nc.scalar.activation(
                out=e_sb[:, :keys], in_=neg_scores[r, m][:, :keys], func=ACT.Exp,
                bias=shifts[r, m][:, 0:1], scale=-1.0, accum_out=e_sums[r][:, m : m + 1],
            )
            e_tiles[r, m] = e_sb

        def row_gain(r):
            if not live(r):
                return
            inv_sum = per_round.tile([P, 2], F32, tag="inv_sum")
            nc.gpsimd.tensor_tensor(out=inv_sum[:], in0=e_sums[r][:], in1=minus_one[:], op=ALU.pow)
            gain = per_round.tile([P, 2], F32, tag="gain")
            nc.gpsimd.tensor_tensor(out=gain[:], in0=inv_sum[:], in1=beta_pair[:], op=ALU.mult)
            gains[r] = gain

        def shape_rows(r, m):
            if not live(r):
                return
            i = query_tiles(r)[m]
            keys = (i + 1) * P
            e_sb, gain = e_tiles[r, m], gains[r][:, m : m + 1]
            shaped = shaped_tiles[i]
            if i > 0:
                nc.vector.tensor_scalar(
                    out=shaped[:, : i * P], in0=e_sb[:, : i * P],
                    scalar1=gain, scalar2=neg_mc[:, i : i + 1],
                    op0=ALU.mult, op1=ALU.add,
                )
            nc.vector.scalar_tensor_tensor(
                out=shaped[:, i * P : keys], in0=e_sb[:, i * P : keys], scalar=gain,
                in1=diag_add[:, i, :], op0=ALU.mult, op1=ALU.add,
            )

        def transpose_shaped(r):
            if not live(r):
                return
            for m in range(2):
                as_f32 = shaped_tiles[query_tiles(r)[m]][:].bitcast(F32)
                for u in range(2):
                    if (m, u) == (0, 1) and r > 0:
                        continue
                    nc.tensor.transpose(pt_ps[:, m, u, :], as_f32[:, u * P : (u + 1) * P], ident_f32[:])
            pt_banks[r] = pt_ps

        def group_shaped(r):
            if not live(r):
                return
            grouped = per_round.tile([P, 2, P, PACK], BF16, tag="grouped", align_bytes=64)
            words_out = grouped[:].rearrange("p m x t -> p (m x t)").bitcast(F32).rearrange("p (m x u) -> p m x u", m=2, u=2)
            words_in = pt_banks[r][:].rearrange("p m u x -> p m x u")
            if r % 4 == 3 or r >= ROUNDS - 4:
                nc.scalar.copy(out=words_out, in_=words_in)
            else:
                nc.vector.tensor_copy(out=words_out, in_=words_in)
            groupeds[r] = grouped

        def quantise_shaped(r):
            if not live(r):
                return
            p_codes = per_round.tile([P, 2 * P], U32, tag="p_codes", align_bytes=64)
            p_scales = per_round.tile([P, 2 * P], U8, tag="p_scales", align_bytes=64)
            nc.vector.quantize_mx(
                out=p_codes[:].bitcast(FP8X4), scales=p_scales[:],
                in_=groupeds[r][:].rearrange("p m x t -> p (m x t)"),
            )
            p_words[r] = (p_codes, p_scales)

        def group_values(r):
            if not live(r):
                return
            n, chunk = divmod(r, 2)
            v_grouped = per_round.tile([P, V_CHUNK, PACK], BF16, tag="v_grouped", align_bytes=64)
            nc.vector.tensor_copy(
                out=v_grouped[:].rearrange("p (c i) t -> p c t i", i=4),
                in_=v_sbs[n][:, :, chunk * V_CHUNK : (chunk + 1) * V_CHUNK].rearrange("p t (c i) -> p c t i", i=4),
            )
            v_groupeds[r] = v_grouped

        def quantise_values(r):
            if not live(r):
                return
            n, chunk = divmod(r, 2)
            if chunk == 0:
                v_codes = per_seq.tile([P, C], U32, tag="v_codes", align_bytes=64)
                v_scales = per_seq.tile([P, C], U8, tag="v_scales", align_bytes=64)
                v_words[n] = (v_codes, v_scales)
            v_codes, v_scales = v_words[n]
            cols = slice(chunk * V_CHUNK, (chunk + 1) * V_CHUNK)
            nc.vector.quantize_mx(
                out=v_codes[:, cols].bitcast(FP8X4), scales=v_scales[:, cols],
                in_=v_groupeds[r][:].rearrange("p c t -> p (c t)"),
            )

        def multiply_values(r):
            if not live(r):
                return
            p_codes, p_scales = p_words[r]
            v_codes, v_scales = v_words[r // 2]
            for m in range(2):
                queries = slice(m * P, (m + 1) * P)
                o_ps = ps_o.tile([P, C], F32, tag="o")
                nc.tensor.matmul_mx(
                    out=o_ps[:],
                    lhsT=p_codes[:, queries].bitcast(FP8X4), lhsT_scale=p_scales[:, queries],
                    rhs=v_codes[:].bitcast(FP8X4), rhs_scale=v_scales[:],
                    start=True, stop=True,
                )
                o_banks[r, m] = o_ps

        def store_output(r, m):
            if not live(r):
                return
            n, i = r // 2, query_tiles(r)[m]
            o_sb = stores.tile([P, C], F32, tag="o_sb")
            if (r, m) == (ROUNDS - 1, 1):
                nc.vector.tensor_copy(out=o_sb[:], in_=o_banks[r, m][:])
            else:
                nc.scalar.copy(out=o_sb[:], in_=o_banks[r, m][:])
            nc.sync.dma_start(out=out[n, i * P : (i + 1) * P, :], in_=o_sb[:])

        def keep_warm(count):
            idle_ps = ps_o.tile([P, C], F32, tag="o")
            for step in range(count):
                nc.tensor.matmul(idle_ps[:], lhsT=zeros[:, :P], rhs=zeros[:], start=True, stop=True)

        def turn(r):
            transpose_inputs(2 * r + 3)
            if -2 < r < 1:
                keep_warm(1)
            transpose_inputs(2 * r + 4)
            if r < 1:
                keep_warm(1)
            scale_and_shift(r - 1, 1)
            quantise_shaped(r - 4)
            quantise_values(r - 1)
            copy_transposed_inputs(2 * r + 3)
            copy_transposed_inputs(2 * r + 4)
            exponentials(r - 1, 1)
            row_gain(r - 1)
            scores(r, 0, (0, 1, 2, 3))
            scale_and_shift(r, 0)
            exponentials(r, 0)
            transpose_shaped(r - 3)
            group_values(r)
            group_shaped(r - 3)
            scores(r, 1, (0, 1))
            multiply_values(r - 4)
            scores(r, 1, (2, 3))
            store_output(r - 4, 0)
            store_output(r - 4, 1)
            shape_rows(r - 2, 0)
            shape_rows(r - 2, 1)

        keep_warm(4)
        for r in range(-2, ROUNDS + 4):
            turn(r)
